import numpy as np
import ml_dtypes

BF16 = ml_dtypes.bfloat16


def bf(x):
    return np.asarray(x, np.float32).astype(BF16)


def f32(x):
    return np.asarray(x, np.float32)


def f64(x):
    return np.asarray(x).astype(np.float64)


def striped(idx):
    return np.tile(idx.reshape(-1, 16).T, (8, 1))


C, S, K, H, N = 128, 4096, 4, 2048, 8192
SHIFT = 0.5


def setup_inputs():
    cat = f32(SHIFT + np.random.standard_normal((C, S)))
    idx = np.concatenate([np.random.permutation(S)[:H] for _ in range(K)])
    return {"cat": cat, "offs": striped(idx)}


def reference(cat, offs):
    idx = offs[:16].T.reshape(-1)
    t = f64(cat)[:, idx].reshape(C, K, H).sum(axis=1)
    mu = t.sum() / t.size
    sd = np.sqrt(np.square(t - mu).sum() / (t.size - 1))
    return (t - mu) / sd

@@ -1,0 +1,56 @@
+import concourse.mybir as mybir
+
+P = 128
+S = 4096
+H = 2048
+K = 4
+COUNT = P * H
+
+F32 = mybir.dt.float32
+U16 = mybir.dt.uint16
+ADD = mybir.AluOpType.add
+MULT = mybir.AluOpType.mult
+ACT = mybir.ActivationFunctionType
+
+
+def tile_core_kernel(tc, cat, offs, out):
+    nc = tc.nc
+    with tc.tile_pool(name="held", bufs=1) as held, tc.psum_pool(name="psum", bufs=1) as psum:
+        offsets = held.tile([P, K * H // 16], U16, name="offsets")
+        nc.sync.dma_start(offsets[:], offs)
+        table = held.tile([P, S], F32, name="table")
+        nc.scalar.dma_start(table[:, 0 : S // 2], cat[:, 0 : S // 2])
+        nc.sync.dma_start(table[:, S // 2 : S], cat[:, S // 2 : S])
+
+        ones = held.tile([P, P], F32, name="ones")
+        nc.gpsimd.memset(ones[:], 1.0)
+
+        t = None
+        for k in range(K):
+            picked = table[:].indirect(offsets[:, k * (H // 16) : (k + 1) * (H // 16)])
+            partial = t
+            t = held.tile([P, H], F32, name=f"t{k}")
+            if k == 0:
+                nc.vector.tensor_copy(t[:], picked)
+            else:
+                nc.vector.tensor_tensor(t[:], picked, partial[:], ADD)
+
+        scratch = held.tile([P, H], F32, name="scratch")
+        rowsum = held.tile([P, 1], F32, name="rowsum")
+        nc.scalar.activation(scratch[:], t[:], ACT.Identity, accum_out=rowsum[:])
+        total = psum.tile([P, 1], F32, name="total")
+        nc.tensor.matmul(total[:], ones[:], rowsum[:], start=True, stop=True)
+        negmean = held.tile([P, 1], F32, name="negmean")
+        nc.vector.tensor_scalar_mul(negmean[:], total[:], -1.0 / COUNT)
+
+        rowsq = held.tile([P, 1], F32, name="rowsq")
+        nc.scalar.activation(scratch[:], t[:], ACT.Square, bias=negmean[:], accum_out=rowsq[:])
+        totalsq = psum.tile([P, 1], F32, name="totalsq")
+        nc.tensor.matmul(totalsq[:], ones[:], rowsq[:], start=True, stop=True)
+        sd = held.tile([P, 1], F32, name="sd")
+        nc.scalar.activation(sd[:], totalsq[:], ACT.Sqrt, scale=1.0 / (COUNT - 1))
+        rstd = held.tile([P, 1], F32, name="rstd")
+        nc.vector.reciprocal(rstd[:], sd[:])
+
+        nc.vector.tensor_scalar(t[:], t[:], negmean[:], rstd[:], ADD, MULT)
+        nc.sync.dma_start(out, t[:])

@@ -4,11 +4,15 @@ P = 128
 S = 4096
 H = 2048
 K = 4
+W = 512
+CHUNKS = H // W
 COUNT = P * H
+VECTOR_W = (2 * W // 3) // 16 * 16
 
 F32 = mybir.dt.float32
 U16 = mybir.dt.uint16
 ADD = mybir.AluOpType.add
+SUBTRACT = mybir.AluOpType.subtract
 MULT = mybir.AluOpType.mult
 ACT = mybir.ActivationFunctionType
 
@@ -22,35 +26,57 @@ def tile_core_kernel(tc, cat, offs, out):
         nc.scalar.dma_start(table[:, 0 : S // 2], cat[:, 0 : S // 2])
         nc.sync.dma_start(table[:, S // 2 : S], cat[:, S // 2 : S])
 
-        ones = held.tile([P, P], F32, name="ones")
-        nc.gpsimd.memset(ones[:], 1.0)
+        averager = held.tile([P, P], F32, name="averager")
+        nc.gpsimd.memset(averager[:], 1.0 / COUNT)
+        warm = held.tile([P, 1], F32, name="warm")
+        nc.scalar.activation(warm[:], averager[:, 0:1], ACT.Sqrt)
 
-        t = None
-        for k in range(K):
-            picked = table[:].indirect(offsets[:, k * (H // 16) : (k + 1) * (H // 16)])
-            partial = t
-            t = held.tile([P, H], F32, name=f"t{k}")
-            if k == 0:
-                nc.vector.tensor_copy(t[:], picked)
-            else:
-                nc.vector.tensor_tensor(t[:], picked, partial[:], ADD)
+        scratch = held.tile([P, W], F32, name="scratch")
+        negshift = held.tile([P, 1], F32, name="negshift")
+        moments = psum.tile([P, 2], F32, name="moments")
+        centred = []
 
-        scratch = held.tile([P, H], F32, name="scratch")
-        rowsum = held.tile([P, 1], F32, name="rowsum")
-        nc.scalar.activation(scratch[:], t[:], ACT.Identity, accum_out=rowsum[:])
-        total = psum.tile([P, 1], F32, name="total")
-        nc.tensor.matmul(total[:], ones[:], rowsum[:], start=True, stop=True)
-        negmean = held.tile([P, 1], F32, name="negmean")
-        nc.vector.tensor_scalar_mul(negmean[:], total[:], -1.0 / COUNT)
+        for i in range(CHUNKS):
+            t = None
+            for k in range(K):
+                first = (k * H + i * W) // 16
+                picked = table[:].indirect(offsets[:, first : first + W // 16])
+                partial = t
+                t = held.tile([P, W], F32, name=f"t{i}_{k}")
+                if k == 0:
+                    nc.vector.tensor_copy(t[:], picked)
+                else:
+                    nc.vector.tensor_tensor(t[:], picked, partial[:], ADD)
 
-        rowsq = held.tile([P, 1], F32, name="rowsq")
-        nc.scalar.activation(scratch[:], t[:], ACT.Square, bias=negmean[:], accum_out=rowsq[:])
-        totalsq = psum.tile([P, 1], F32, name="totalsq")
-        nc.tensor.matmul(totalsq[:], ones[:], rowsq[:], start=True, stop=True)
-        sd = held.tile([P, 1], F32, name="sd")
-        nc.scalar.activation(sd[:], totalsq[:], ACT.Sqrt, scale=1.0 / (COUNT - 1))
+            if i == 0:
+                rowsum = held.tile([P, 1], F32, name="rowsum")
+                nc.scalar.activation(scratch[:], t[:], ACT.Identity, accum_out=rowsum[:])
+                share = psum.tile([P, 1], F32, name="share")
+                nc.tensor.matmul(share[:], averager[:], rowsum[:], start=True, stop=True)
+                nc.scalar.activation(negshift[:], share[:], ACT.Copy, scale=-1.0 * CHUNKS)
+
+            d = held.tile([P, W], F32, name=f"d{i}")
+            rows = held.tile([P, 2], F32, name=f"rows{i}")
+            nc.scalar.activation(d[:], t[:], ACT.Identity, bias=negshift[:], accum_out=rows[:, 0:1])
+            nc.scalar.activation(scratch[:], d[:], ACT.Square, accum_out=rows[:, 1:2])
+            nc.tensor.matmul(moments[:], averager[:], rows[:], start=(i == 0), stop=(i == CHUNKS - 1))
+            centred.append(d)
+
+        m1 = held.tile([P, 1], F32, name="m1")
+        negvar = held.tile([P, 1], F32, name="negvar")
+        inverse = held.tile([P, 1], F32, name="inverse")
+        negm1 = held.tile([P, 1], F32, name="negm1")
         rstd = held.tile([P, 1], F32, name="rstd")
-        nc.vector.reciprocal(rstd[:], sd[:])
+        offset = held.tile([P, 1], F32, name="offset")
+        nc.vector.tensor_scalar(negvar[:], moments[:, 0:1], moments[:, 0:1], moments[:, 1:2], MULT, SUBTRACT)
+        nc.vector.reciprocal(inverse[:], negvar[:])
+        nc.vector.tensor_copy(m1[:], moments[:, 0:1])
+        nc.vector.tensor_scalar_mul(negm1[:], moments[:, 0:1], -1.0)
+        nc.scalar.activation(rstd[:], inverse[:], ACT.Sqrt, scale=-1.0 * (COUNT - 1) / COUNT)
+        nc.scalar.activation(offset[:], negm1[:], ACT.Identity, scale=rstd[:])
 
-        nc.vector.tensor_scalar(t[:], t[:], negmean[:], rstd[:], ADD, MULT)
-        nc.sync.dma_start(out, t[:])
+        for i in range(CHUNKS):
+            d = centred[i]
+            nc.vector.tensor_scalar(d[:, 0:VECTOR_W], d[:, 0:VECTOR_W], m1[:], rstd[:], SUBTRACT, MULT)
+            nc.scalar.activation(d[:, VECTOR_W:W], d[:, VECTOR_W:W], ACT.Identity, bias=offset[:], scale=rstd[:])
+            nc.sync.dma_start(out[:, i * W : (i + 1) * W], d[:])

@@ -33,7 +33,8 @@ def tile_core_kernel(tc, cat, offs, out):
 
         scratch = held.tile([P, W], F32, name="scratch")
         negshift = held.tile([P, 1], F32, name="negshift")
-        moments = psum.tile([P, 2], F32, name="moments")
+        m1_sum = psum.tile([P, 1], F32, name="m1_sum")
+        m2_sum = psum.tile([P, 1], F32, name="m2_sum")
         centred = []
 
         for i in range(CHUNKS):
@@ -55,11 +56,17 @@ def tile_core_kernel(tc, cat, offs, out):
                 nc.tensor.matmul(share[:], averager[:], rowsum[:], start=True, stop=True)
                 nc.scalar.activation(negshift[:], share[:], ACT.Copy, scale=-1.0 * CHUNKS)
 
+            first_chunk, last_chunk = i == 0, i == CHUNKS - 1
             d = held.tile([P, W], F32, name=f"d{i}")
-            rows = held.tile([P, 2], F32, name=f"rows{i}")
-            nc.scalar.activation(d[:], t[:], ACT.Identity, bias=negshift[:], accum_out=rows[:, 0:1])
-            nc.scalar.activation(scratch[:], d[:], ACT.Square, accum_out=rows[:, 1:2])
-            nc.tensor.matmul(moments[:], averager[:], rows[:], start=(i == 0), stop=(i == CHUNKS - 1))
+            rowsum_d = held.tile([P, 1], F32, name=f"rowsum_d{i}")
+            rowsum_dd = held.tile([P, 1], F32, name=f"rowsum_dd{i}")
+            if last_chunk:
+                nc.vector.tensor_scalar(d[:], t[:], negshift[:], None, ADD, ADD, accum_out=rowsum_d[:])
+            else:
+                nc.scalar.activation(d[:], t[:], ACT.Identity, bias=negshift[:], accum_out=rowsum_d[:])
+            nc.scalar.activation(scratch[:], t[:], ACT.Square, bias=negshift[:], accum_out=rowsum_dd[:])
+            nc.tensor.matmul(m1_sum[:], averager[:], rowsum_d[:], start=first_chunk, stop=last_chunk)
+            nc.tensor.matmul(m2_sum[:], averager[:], rowsum_dd[:], start=first_chunk, stop=last_chunk)
             centred.append(d)
 
         m1 = held.tile([P, 1], F32, name="m1")
@@ -68,10 +75,10 @@ def tile_core_kernel(tc, cat, offs, out):
         negm1 = held.tile([P, 1], F32, name="negm1")
         rstd = held.tile([P, 1], F32, name="rstd")
         offset = held.tile([P, 1], F32, name="offset")
-        nc.vector.tensor_scalar(negvar[:], moments[:, 0:1], moments[:, 0:1], moments[:, 1:2], MULT, SUBTRACT)
+        nc.vector.tensor_scalar(negvar[:], m1_sum[:], m1_sum[:], m2_sum[:], MULT, SUBTRACT)
         nc.vector.reciprocal(inverse[:], negvar[:])
-        nc.vector.tensor_copy(m1[:], moments[:, 0:1])
-        nc.vector.tensor_scalar_mul(negm1[:], moments[:, 0:1], -1.0)
+        nc.vector.tensor_copy(m1[:], m1_sum[:])
+        nc.vector.tensor_scalar_mul(negm1[:], m1_sum[:], -1.0)
         nc.scalar.activation(rstd[:], inverse[:], ACT.Sqrt, scale=-1.0 * (COUNT - 1) / COUNT)
         nc.scalar.activation(offset[:], negm1[:], ACT.Identity, scale=rstd[:])
 

@@ -8,6 +8,7 @@ W = 512
 CHUNKS = H // W
 COUNT = P * H
 VECTOR_W = (2 * W // 3) // 16 * 16
+LINE = 8
 
 F32 = mybir.dt.float32
 U16 = mybir.dt.uint16
@@ -29,12 +30,11 @@ def tile_core_kernel(tc, cat, offs, out):
         averager = held.tile([P, P], F32, name="averager")
         nc.gpsimd.memset(averager[:], 1.0 / COUNT)
         warm = held.tile([P, 1], F32, name="warm")
-        nc.scalar.activation(warm[:], averager[:, 0:1], ACT.Sqrt)
+        nc.scalar.activation(warm[:], averager[:, 0:1], ACT.Abs_reciprocal_sqrt)
 
         scratch = held.tile([P, W], F32, name="scratch")
         negshift = held.tile([P, 1], F32, name="negshift")
-        m1_sum = psum.tile([P, 1], F32, name="m1_sum")
-        m2_sum = psum.tile([P, 1], F32, name="m2_sum")
+        moments = psum.tile([P, 2], F32, name="moments")
         centred = []
 
         for i in range(CHUNKS):
@@ -58,28 +58,26 @@ def tile_core_kernel(tc, cat, offs, out):
 
             first_chunk, last_chunk = i == 0, i == CHUNKS - 1
             d = held.tile([P, W], F32, name=f"d{i}")
-            rowsum_d = held.tile([P, 1], F32, name=f"rowsum_d{i}")
-            rowsum_dd = held.tile([P, 1], F32, name=f"rowsum_dd{i}")
+            rows = held.tile([P, 2 * LINE], F32, name=f"rows{i}")
+            rowsum_d, rowsum_dd = rows[:, 0:1], rows[:, LINE : LINE + 1]
             if last_chunk:
-                nc.vector.tensor_scalar(d[:], t[:], negshift[:], None, ADD, ADD, accum_out=rowsum_d[:])
+                nc.vector.tensor_scalar(d[:], t[:], negshift[:], None, ADD, ADD, accum_out=rowsum_d)
             else:
-                nc.scalar.activation(d[:], t[:], ACT.Identity, bias=negshift[:], accum_out=rowsum_d[:])
-            nc.scalar.activation(scratch[:], t[:], ACT.Square, bias=negshift[:], accum_out=rowsum_dd[:])
-            nc.tensor.matmul(m1_sum[:], averager[:], rowsum_d[:], start=first_chunk, stop=last_chunk)
-            nc.tensor.matmul(m2_sum[:], averager[:], rowsum_dd[:], start=first_chunk, stop=last_chunk)
+                nc.scalar.activation(d[:], t[:], ACT.Identity, bias=negshift[:], accum_out=rowsum_d)
+            nc.scalar.activation(scratch[:], t[:], ACT.Square, bias=negshift[:], accum_out=rowsum_dd)
+            both = rows[:].rearrange("p (m line) -> p m line", line=LINE)[:, :, 0]
+            nc.tensor.matmul(moments[:], averager[:], both, start=first_chunk, stop=last_chunk)
             centred.append(d)
 
         m1 = held.tile([P, 1], F32, name="m1")
         negvar = held.tile([P, 1], F32, name="negvar")
-        inverse = held.tile([P, 1], F32, name="inverse")
         negm1 = held.tile([P, 1], F32, name="negm1")
         rstd = held.tile([P, 1], F32, name="rstd")
         offset = held.tile([P, 1], F32, name="offset")
-        nc.vector.tensor_scalar(negvar[:], m1_sum[:], m1_sum[:], m2_sum[:], MULT, SUBTRACT)
-        nc.vector.reciprocal(inverse[:], negvar[:])
-        nc.vector.tensor_copy(m1[:], m1_sum[:])
-        nc.vector.tensor_scalar_mul(negm1[:], m1_sum[:], -1.0)
-        nc.scalar.activation(rstd[:], inverse[:], ACT.Sqrt, scale=-1.0 * (COUNT - 1) / COUNT)
+        nc.vector.tensor_scalar(negvar[:], moments[:, 0:1], moments[:, 0:1], moments[:, 1:2], MULT, SUBTRACT)
+        nc.vector.tensor_copy(m1[:], moments[:, 0:1])
+        nc.vector.tensor_scalar_mul(negm1[:], moments[:, 0:1], -1.0)
+        nc.scalar.activation(rstd[:], negvar[:], ACT.Abs_reciprocal_sqrt, scale=1.0 * COUNT / (COUNT - 1))
         nc.scalar.activation(offset[:], negm1[:], ACT.Identity, scale=rstd[:])
 
         for i in range(CHUNKS):

@@ -8,7 +8,7 @@ W = 512
 CHUNKS = H // W
 COUNT = P * H
 VECTOR_W = (2 * W // 3) // 16 * 16
-LINE = 8
+BLOCK = 8
 
 F32 = mybir.dt.float32
 U16 = mybir.dt.uint16
@@ -32,16 +32,18 @@ def tile_core_kernel(tc, cat, offs, out):
         warm = held.tile([P, 1], F32, name="warm")
         nc.scalar.activation(warm[:], averager[:, 0:1], ACT.Abs_reciprocal_sqrt)
 
-        scratch = held.tile([P, W], F32, name="scratch")
+        unread = held.tile([P, W], F32, name="unread")
         negshift = held.tile([P, 1], F32, name="negshift")
         moments = psum.tile([P, 2], F32, name="moments")
         centred = []
 
         for i in range(CHUNKS):
+            first_chunk, last_chunk = i == 0, i == CHUNKS - 1
+
             t = None
             for k in range(K):
-                first = (k * H + i * W) // 16
-                picked = table[:].indirect(offsets[:, first : first + W // 16])
+                column = (k * H + i * W) // 16
+                picked = table[:].indirect(offsets[:, column : column + W // 16])
                 partial = t
                 t = held.tile([P, W], F32, name=f"t{i}_{k}")
                 if k == 0:
@@ -49,39 +51,37 @@ def tile_core_kernel(tc, cat, offs, out):
                 else:
                     nc.vector.tensor_tensor(t[:], picked, partial[:], ADD)
 
-            if i == 0:
-                rowsum = held.tile([P, 1], F32, name="rowsum")
-                nc.scalar.activation(scratch[:], t[:], ACT.Identity, accum_out=rowsum[:])
+            if first_chunk:
+                rowsum_t = held.tile([P, 1], F32, name="rowsum_t")
+                nc.scalar.activation(unread[:], t[:], ACT.Identity, accum_out=rowsum_t[:])
                 share = psum.tile([P, 1], F32, name="share")
-                nc.tensor.matmul(share[:], averager[:], rowsum[:], start=True, stop=True)
+                nc.tensor.matmul(share[:], averager[:], rowsum_t[:], start=True, stop=True)
                 nc.scalar.activation(negshift[:], share[:], ACT.Copy, scale=-1.0 * CHUNKS)
 
-            first_chunk, last_chunk = i == 0, i == CHUNKS - 1
             d = held.tile([P, W], F32, name=f"d{i}")
-            rows = held.tile([P, 2 * LINE], F32, name=f"rows{i}")
-            rowsum_d, rowsum_dd = rows[:, 0:1], rows[:, LINE : LINE + 1]
+            rowsums = held.tile([P, 2 * BLOCK], F32, name=f"rowsums{i}")
+            rowsum_d, rowsum_dd = rowsums[:, 0:1], rowsums[:, BLOCK : BLOCK + 1]
             if last_chunk:
                 nc.vector.tensor_scalar(d[:], t[:], negshift[:], None, ADD, ADD, accum_out=rowsum_d)
             else:
                 nc.scalar.activation(d[:], t[:], ACT.Identity, bias=negshift[:], accum_out=rowsum_d)
-            nc.scalar.activation(scratch[:], t[:], ACT.Square, bias=negshift[:], accum_out=rowsum_dd)
-            both = rows[:].rearrange("p (m line) -> p m line", line=LINE)[:, :, 0]
-            nc.tensor.matmul(moments[:], averager[:], both, start=first_chunk, stop=last_chunk)
+            nc.scalar.activation(unread[:], t[:], ACT.Square, bias=negshift[:], accum_out=rowsum_dd)
             centred.append(d)
 
-        m1 = held.tile([P, 1], F32, name="m1")
-        negvar = held.tile([P, 1], F32, name="negvar")
-        negm1 = held.tile([P, 1], F32, name="negm1")
-        rstd = held.tile([P, 1], F32, name="rstd")
-        offset = held.tile([P, 1], F32, name="offset")
-        nc.vector.tensor_scalar(negvar[:], moments[:, 0:1], moments[:, 0:1], moments[:, 1:2], MULT, SUBTRACT)
-        nc.vector.tensor_copy(m1[:], moments[:, 0:1])
-        nc.vector.tensor_scalar_mul(negm1[:], moments[:, 0:1], -1.0)
-        nc.scalar.activation(rstd[:], negvar[:], ACT.Abs_reciprocal_sqrt, scale=1.0 * COUNT / (COUNT - 1))
-        nc.scalar.activation(offset[:], negm1[:], ACT.Identity, scale=rstd[:])
+            both = rowsums[:].rearrange("p (m block) -> p m block", block=BLOCK)[:, :, 0]
+            nc.tensor.matmul(moments[:], averager[:], both, start=first_chunk, stop=last_chunk)
 
+        negvar = held.tile([P, 1], F32, name="negvar")
+        nc.vector.tensor_scalar(negvar[:], moments[:, 0:1], moments[:, 0:1], moments[:, 1:2], MULT, SUBTRACT)
+        rstd = held.tile([P, 1], F32, name="rstd")
+        nc.scalar.activation(rstd[:], negvar[:], ACT.Abs_reciprocal_sqrt, scale=COUNT / (COUNT - 1))
+        negm1 = held.tile([P, 1], F32, name="negm1")
+        nc.vector.tensor_scalar_mul(negm1[:], moments[:, 0:1], -1.0)
+
+        negm1_rstd = held.tile([P, 1], F32, name="negm1_rstd")
+        nc.scalar.activation(negm1_rstd[:], negm1[:], ACT.Identity, scale=rstd[:])
         for i in range(CHUNKS):
             d = centred[i]
-            nc.vector.tensor_scalar(d[:, 0:VECTOR_W], d[:, 0:VECTOR_W], m1[:], rstd[:], SUBTRACT, MULT)
-            nc.scalar.activation(d[:, VECTOR_W:W], d[:, VECTOR_W:W], ACT.Identity, bias=offset[:], scale=rstd[:])
+            nc.vector.tensor_scalar(d[:, 0:VECTOR_W], d[:, 0:VECTOR_W], negm1[:], rstd[:], ADD, MULT)
+            nc.scalar.activation(d[:, VECTOR_W:W], d[:, VECTOR_W:W], ACT.Identity, bias=negm1_rstd[:], scale=rstd[:])
             nc.sync.dma_start(out[:, i * W : (i + 1) * W], d[:])

@@ -4,10 +4,12 @@ P = 128
 S = 4096
 H = 2048
 K = 4
-W = 512
-CHUNKS = H // W
 COUNT = P * H
-VECTOR_W = (2 * W // 3) // 16 * 16
+WIDE = 1536
+NARROW = H - WIDE
+LANES = 2
+PIECE = 512
+VECTOR_W = (2 * PIECE // 3) // 16 * 16
 BLOCK = 8
 
 F32 = mybir.dt.float32
@@ -29,59 +31,74 @@ def tile_core_kernel(tc, cat, offs, out):
 
         averager = held.tile([P, P], F32, name="averager")
         nc.gpsimd.memset(averager[:], 1.0 / COUNT)
+        zeros = held.tile([P, WIDE // LANES], F32, name="zeros")
+        nc.gpsimd.memset(zeros[:], 0.0)
         warm = held.tile([P, 1], F32, name="warm")
         nc.scalar.activation(warm[:], averager[:, 0:1], ACT.Abs_reciprocal_sqrt)
 
-        unread = held.tile([P, W], F32, name="unread")
-        negshift = held.tile([P, 1], F32, name="negshift")
-        moments = psum.tile([P, 2], F32, name="moments")
-        centred = []
-
-        for i in range(CHUNKS):
-            first_chunk, last_chunk = i == 0, i == CHUNKS - 1
-
-            t = None
+        def gathered_sum(name, first, width):
+            t = held.tile([P, width], F32, name=name)
+            lane_w = width // LANES
+            sums = [zeros[:, 0:lane_w]] * LANES
             for k in range(K):
-                column = (k * H + i * W) // 16
-                picked = table[:].indirect(offsets[:, column : column + W // 16])
-                partial = t
-                t = held.tile([P, W], F32, name=f"t{i}_{k}")
-                if k == 0:
-                    nc.vector.tensor_copy(t[:], picked)
-                else:
-                    nc.vector.tensor_tensor(t[:], picked, partial[:], ADD)
+                for lane in range(LANES):
+                    column = (k * H + first + lane * lane_w) // 16
+                    picked = table[:].indirect(offsets[:, column : column + lane_w // 16])
+                    if k < K - 1:
+                        partial = held.tile([P, lane_w], F32, name=f"{name}_{lane}_{k}")
+                        longer = partial[:]
+                    else:
+                        longer = t[:, lane * lane_w : (lane + 1) * lane_w]
+                    nc.vector.tensor_tensor(longer, picked, sums[lane], ADD)
+                    sums[lane] = longer
+            return t
 
-            if first_chunk:
-                rowsum_t = held.tile([P, 1], F32, name="rowsum_t")
-                nc.scalar.activation(unread[:], t[:], ACT.Identity, accum_out=rowsum_t[:])
-                share = psum.tile([P, 1], F32, name="share")
-                nc.tensor.matmul(share[:], averager[:], rowsum_t[:], start=True, stop=True)
-                nc.scalar.activation(negshift[:], share[:], ACT.Copy, scale=-1.0 * CHUNKS)
+        moments = psum.tile([P, 2], F32, name="moments")
+        scalar_unread = held.tile([P, WIDE], F32, name="scalar_unread")
+        vector_unread = held.tile([P, NARROW], F32, name="vector_unread")
 
-            d = held.tile([P, W], F32, name=f"d{i}")
-            rowsums = held.tile([P, 2 * BLOCK], F32, name=f"rowsums{i}")
-            rowsum_d, rowsum_dd = rowsums[:, 0:1], rowsums[:, BLOCK : BLOCK + 1]
-            if last_chunk:
-                nc.vector.tensor_scalar(d[:], t[:], negshift[:], None, ADD, ADD, accum_out=rowsum_d)
-            else:
-                nc.scalar.activation(d[:], t[:], ACT.Identity, bias=negshift[:], accum_out=rowsum_d)
-            nc.scalar.activation(unread[:], t[:], ACT.Square, bias=negshift[:], accum_out=rowsum_dd)
-            centred.append(d)
+        t_wide = gathered_sum("t_wide", 0, WIDE)
+        rowsum_t = held.tile([P, 1], F32, name="rowsum_t")
+        nc.scalar.activation(scalar_unread[:], t_wide[:], ACT.Identity, accum_out=rowsum_t[:])
+        share = psum.tile([P, 1], F32, name="share")
+        nc.tensor.matmul(share[:], averager[:], rowsum_t[:], start=True, stop=True)
+        negshift = held.tile([P, 1], F32, name="negshift")
+        nc.scalar.activation(negshift[:], share[:], ACT.Copy, scale=-1.0 * H / WIDE)
+        rowsums_wide = held.tile([P, 2 * BLOCK], F32, name="rowsums_wide")
+        nc.gpsimd.memset(rowsums_wide[:], 0.0)
+        nc.scalar.activation(
+            scalar_unread[:], t_wide[:], ACT.Square, bias=negshift[:], accum_out=rowsums_wide[:, BLOCK : BLOCK + 1]
+        )
+        both = rowsums_wide[:].rearrange("p (m block) -> p m block", block=BLOCK)[:, :, 0]
+        nc.tensor.matmul(moments[:], averager[:], both, start=True, stop=False)
 
-            both = rowsums[:].rearrange("p (m block) -> p m block", block=BLOCK)[:, :, 0]
-            nc.tensor.matmul(moments[:], averager[:], both, start=first_chunk, stop=last_chunk)
+        t_narrow = gathered_sum("t_narrow", WIDE, NARROW)
+        rowsums_narrow = held.tile([P, 2 * BLOCK], F32, name="rowsums_narrow")
+        nc.vector.tensor_scalar(
+            vector_unread[:], t_narrow[:], negshift[:], None, ADD, ADD, accum_out=rowsums_narrow[:, 0:1]
+        )
+        nc.scalar.activation(
+            scalar_unread[:, 0:NARROW],
+            t_narrow[:],
+            ACT.Square,
+            bias=negshift[:],
+            accum_out=rowsums_narrow[:, BLOCK : BLOCK + 1],
+        )
+        both = rowsums_narrow[:].rearrange("p (m block) -> p m block", block=BLOCK)[:, :, 0]
+        nc.tensor.matmul(moments[:], averager[:], both, start=False, stop=True)
 
         negvar = held.tile([P, 1], F32, name="negvar")
         nc.vector.tensor_scalar(negvar[:], moments[:, 0:1], moments[:, 0:1], moments[:, 1:2], MULT, SUBTRACT)
         rstd = held.tile([P, 1], F32, name="rstd")
         nc.scalar.activation(rstd[:], negvar[:], ACT.Abs_reciprocal_sqrt, scale=COUNT / (COUNT - 1))
-        negm1 = held.tile([P, 1], F32, name="negm1")
-        nc.vector.tensor_scalar_mul(negm1[:], moments[:, 0:1], -1.0)
+        negmu = held.tile([P, 1], F32, name="negmu")
+        nc.vector.tensor_tensor(negmu[:], negshift[:], moments[:, 0:1], SUBTRACT)
 
-        negm1_rstd = held.tile([P, 1], F32, name="negm1_rstd")
-        nc.scalar.activation(negm1_rstd[:], negm1[:], ACT.Identity, scale=rstd[:])
-        for i in range(CHUNKS):
-            d = centred[i]
-            nc.vector.tensor_scalar(d[:, 0:VECTOR_W], d[:, 0:VECTOR_W], negm1[:], rstd[:], ADD, MULT)
-            nc.scalar.activation(d[:, VECTOR_W:W], d[:, VECTOR_W:W], ACT.Identity, bias=negm1_rstd[:], scale=rstd[:])
-            nc.sync.dma_start(out[:, i * W : (i + 1) * W], d[:])
+        negmu_rstd = held.tile([P, 1], F32, name="negmu_rstd")
+        nc.scalar.activation(negmu_rstd[:], negmu[:], ACT.Identity, scale=rstd[:])
+        for t, first, width in ((t_wide, 0, WIDE), (t_narrow, WIDE, NARROW)):
+            for a in range(0, width, PIECE):
+                b, c = a + VECTOR_W, a + PIECE
+                nc.vector.tensor_scalar(t[:, a:b], t[:, a:b], negmu[:], rstd[:], ADD, MULT)
+                nc.scalar.activation(t[:, b:c], t[:, b:c], ACT.Identity, bias=negmu_rstd[:], scale=rstd[:])
+                nc.sync.dma_start(out[:, first + a : first + c], t[:, a:c])

@@ -5,11 +5,9 @@ S = 4096
 H = 2048
 K = 4
 COUNT = P * H
-WIDE = 1536
-NARROW = H - WIDE
-LANES = 2
-PIECE = 512
-VECTOR_W = (2 * PIECE // 3) // 16 * 16
+WIDTHS = (768, 768, 256, 256)
+CHUNKS = len(WIDTHS)
+STARTS = [sum(WIDTHS[:i]) for i in range(CHUNKS)]
 BLOCK = 8
 
 F32 = mybir.dt.float32
@@ -31,61 +29,47 @@ def tile_core_kernel(tc, cat, offs, out):
 
         averager = held.tile([P, P], F32, name="averager")
         nc.gpsimd.memset(averager[:], 1.0 / COUNT)
-        zeros = held.tile([P, WIDE // LANES], F32, name="zeros")
+        zeros = held.tile([P, max(WIDTHS)], F32, name="zeros")
         nc.gpsimd.memset(zeros[:], 0.0)
         warm = held.tile([P, 1], F32, name="warm")
         nc.scalar.activation(warm[:], averager[:, 0:1], ACT.Abs_reciprocal_sqrt)
 
-        def gathered_sum(name, first, width):
-            t = held.tile([P, width], F32, name=name)
-            lane_w = width // LANES
-            sums = [zeros[:, 0:lane_w]] * LANES
-            for k in range(K):
-                for lane in range(LANES):
-                    column = (k * H + first + lane * lane_w) // 16
-                    picked = table[:].indirect(offsets[:, column : column + lane_w // 16])
-                    if k < K - 1:
-                        partial = held.tile([P, lane_w], F32, name=f"{name}_{lane}_{k}")
-                        longer = partial[:]
-                    else:
-                        longer = t[:, lane * lane_w : (lane + 1) * lane_w]
-                    nc.vector.tensor_tensor(longer, picked, sums[lane], ADD)
-                    sums[lane] = longer
-            return t
-
-        moments = psum.tile([P, 2], F32, name="moments")
-        scalar_unread = held.tile([P, WIDE], F32, name="scalar_unread")
-        vector_unread = held.tile([P, NARROW], F32, name="vector_unread")
-
-        t_wide = gathered_sum("t_wide", 0, WIDE)
-        rowsum_t = held.tile([P, 1], F32, name="rowsum_t")
-        nc.scalar.activation(scalar_unread[:], t_wide[:], ACT.Identity, accum_out=rowsum_t[:])
-        share = psum.tile([P, 1], F32, name="share")
-        nc.tensor.matmul(share[:], averager[:], rowsum_t[:], start=True, stop=True)
+        scalar_unread = held.tile([P, max(WIDTHS)], F32, name="scalar_unread")
+        vector_unread = held.tile([P, WIDTHS[-1]], F32, name="vector_unread")
         negshift = held.tile([P, 1], F32, name="negshift")
-        nc.scalar.activation(negshift[:], share[:], ACT.Copy, scale=-1.0 * H / WIDE)
-        rowsums_wide = held.tile([P, 2 * BLOCK], F32, name="rowsums_wide")
-        nc.gpsimd.memset(rowsums_wide[:], 0.0)
-        nc.scalar.activation(
-            scalar_unread[:], t_wide[:], ACT.Square, bias=negshift[:], accum_out=rowsums_wide[:, BLOCK : BLOCK + 1]
-        )
-        both = rowsums_wide[:].rearrange("p (m block) -> p m block", block=BLOCK)[:, :, 0]
-        nc.tensor.matmul(moments[:], averager[:], both, start=True, stop=False)
+        moments = psum.tile([P, 2], F32, name="moments")
 
-        t_narrow = gathered_sum("t_narrow", WIDE, NARROW)
-        rowsums_narrow = held.tile([P, 2 * BLOCK], F32, name="rowsums_narrow")
-        nc.vector.tensor_scalar(
-            vector_unread[:], t_narrow[:], negshift[:], None, ADD, ADD, accum_out=rowsums_narrow[:, 0:1]
-        )
-        nc.scalar.activation(
-            scalar_unread[:, 0:NARROW],
-            t_narrow[:],
-            ACT.Square,
-            bias=negshift[:],
-            accum_out=rowsums_narrow[:, BLOCK : BLOCK + 1],
-        )
-        both = rowsums_narrow[:].rearrange("p (m block) -> p m block", block=BLOCK)[:, :, 0]
-        nc.tensor.matmul(moments[:], averager[:], both, start=False, stop=True)
+        def statistics(i, t):
+            first_chunk, last_chunk = i == 0, i == CHUNKS - 1
+            unread = scalar_unread[:, 0 : WIDTHS[i]]
+            rowsums = held.tile([P, 2 * BLOCK], F32, name=f"rowsums{i}")
+            rowsum_d, rowsum_dd = rowsums[:, 0:1], rowsums[:, BLOCK : BLOCK + 1]
+            if first_chunk:
+                rowsum_t = held.tile([P, 1], F32, name="rowsum_t")
+                nc.scalar.activation(unread, t, ACT.Identity, accum_out=rowsum_t[:])
+                share = psum.tile([P, 1], F32, name="share")
+                nc.tensor.matmul(share[:], averager[:], rowsum_t[:], start=True, stop=True)
+                nc.scalar.activation(negshift[:], share[:], ACT.Copy, scale=-1.0 * H / WIDTHS[0])
+                nc.gpsimd.memset(rowsums[:], 0.0)
+            elif last_chunk:
+                nc.vector.tensor_scalar(vector_unread[:], t, negshift[:], None, ADD, ADD, accum_out=rowsum_d)
+            else:
+                nc.scalar.activation(unread, t, ACT.Identity, bias=negshift[:], accum_out=rowsum_d)
+            nc.scalar.activation(unread, t, ACT.Square, bias=negshift[:], accum_out=rowsum_dd)
+            both = rowsums[:].rearrange("p (m block) -> p m block", block=BLOCK)[:, :, 0]
+            nc.tensor.matmul(moments[:], averager[:], both, start=first_chunk, stop=last_chunk)
+
+        sums = [zeros[:, 0:width] for width in WIDTHS]
+        for pair in range(0, CHUNKS, 2):
+            for k in range(K):
+                for i in (pair, pair + 1):
+                    column = (k * H + STARTS[i]) // 16
+                    picked = table[:].indirect(offsets[:, column : column + WIDTHS[i] // 16])
+                    longer = held.tile([P, WIDTHS[i]], F32, name=f"t{i}_{k}")
+                    nc.vector.tensor_tensor(longer[:], picked, sums[i], ADD)
+                    sums[i] = longer[:]
+            statistics(pair, sums[pair])
+            statistics(pair + 1, sums[pair + 1])
 
         negvar = held.tile([P, 1], F32, name="negvar")
         nc.vector.tensor_scalar(negvar[:], moments[:, 0:1], moments[:, 0:1], moments[:, 1:2], MULT, SUBTRACT)
@@ -94,11 +78,6 @@ def tile_core_kernel(tc, cat, offs, out):
         negmu = held.tile([P, 1], F32, name="negmu")
         nc.vector.tensor_tensor(negmu[:], negshift[:], moments[:, 0:1], SUBTRACT)
 
-        negmu_rstd = held.tile([P, 1], F32, name="negmu_rstd")
-        nc.scalar.activation(negmu_rstd[:], negmu[:], ACT.Identity, scale=rstd[:])
-        for t, first, width in ((t_wide, 0, WIDE), (t_narrow, WIDE, NARROW)):
-            for a in range(0, width, PIECE):
-                b, c = a + VECTOR_W, a + PIECE
-                nc.vector.tensor_scalar(t[:, a:b], t[:, a:b], negmu[:], rstd[:], ADD, MULT)
-                nc.scalar.activation(t[:, b:c], t[:, b:c], ACT.Identity, bias=negmu_rstd[:], scale=rstd[:])
-                nc.sync.dma_start(out[:, first + a : first + c], t[:, a:c])
+        for i in reversed(range(CHUNKS)):
+            nc.vector.tensor_scalar(sums[i], sums[i], negmu[:], rstd[:], ADD, MULT)
+            nc.sync.dma_start(out[:, STARTS[i] : STARTS[i] + WIDTHS[i]], sums[i])

@@ -9,6 +9,7 @@ WIDTHS = (768, 768, 256, 256)
 CHUNKS = len(WIDTHS)
 STARTS = [sum(WIDTHS[:i]) for i in range(CHUNKS)]
 BLOCK = 8
+QUADRANT = 32
 
 F32 = mybir.dt.float32
 U16 = mybir.dt.uint16
@@ -27,8 +28,12 @@ def tile_core_kernel(tc, cat, offs, out):
         nc.scalar.dma_start(table[:, 0 : S // 2], cat[:, 0 : S // 2])
         nc.sync.dma_start(table[:, S // 2 : S], cat[:, S // 2 : S])
 
-        averager = held.tile([P, P], F32, name="averager")
+        averager = held.tile([P, QUADRANT], F32, name="averager")
         nc.gpsimd.memset(averager[:], 1.0 / COUNT)
+
+        def average(result, rowsums, start, stop):
+            for q in range(0, P, QUADRANT):
+                nc.tensor.matmul(result[q : q + QUADRANT, :], averager[:], rowsums, start=start, stop=stop)
         zeros = held.tile([P, max(WIDTHS)], F32, name="zeros")
         nc.gpsimd.memset(zeros[:], 0.0)
         warm = held.tile([P, 1], F32, name="warm")
@@ -48,7 +53,7 @@ def tile_core_kernel(tc, cat, offs, out):
                 rowsum_t = held.tile([P, 1], F32, name="rowsum_t")
                 nc.scalar.activation(unread, t, ACT.Identity, accum_out=rowsum_t[:])
                 share = psum.tile([P, 1], F32, name="share")
-                nc.tensor.matmul(share[:], averager[:], rowsum_t[:], start=True, stop=True)
+                average(share, rowsum_t[:], True, True)
                 nc.scalar.activation(negshift[:], share[:], ACT.Copy, scale=-1.0 * H / WIDTHS[0])
                 nc.gpsimd.memset(rowsums[:], 0.0)
             elif last_chunk:
@@ -57,7 +62,7 @@ def tile_core_kernel(tc, cat, offs, out):
                 nc.scalar.activation(unread, t, ACT.Identity, bias=negshift[:], accum_out=rowsum_d)
             nc.scalar.activation(unread, t, ACT.Square, bias=negshift[:], accum_out=rowsum_dd)
             both = rowsums[:].rearrange("p (m block) -> p m block", block=BLOCK)[:, :, 0]
-            nc.tensor.matmul(moments[:], averager[:], both, start=first_chunk, stop=last_chunk)
+            average(moments, both, first_chunk, last_chunk)
 
         sums = [zeros[:, 0:width] for width in WIDTHS]
         for pair in range(0, CHUNKS, 2):

@@ -5,7 +5,7 @@ S = 4096
 H = 2048
 K = 4
 COUNT = P * H
-WIDTHS = (768, 768, 256, 256)
+WIDTHS = (768, 768, 192, 320)
 CHUNKS = len(WIDTHS)
 STARTS = [sum(WIDTHS[:i]) for i in range(CHUNKS)]
 BLOCK = 8

@@ -5,10 +5,12 @@ S = 4096
 H = 2048
 K = 4
 COUNT = P * H
-WIDTHS = (768, 768, 192, 320)
+BESSEL = COUNT / (COUNT - 1)
+WIDTHS = (640, 1024, 256, 128)
+LAST_PAIR = len(WIDTHS) - 2
 CHUNKS = len(WIDTHS)
+PIECES = (256, 384, 640, 768)
 STARTS = [sum(WIDTHS[:i]) for i in range(CHUNKS)]
-BLOCK = 8
 QUADRANT = 32
 
 F32 = mybir.dt.float32
@@ -40,49 +42,58 @@ def tile_core_kernel(tc, cat, offs, out):
         nc.scalar.activation(warm[:], averager[:, 0:1], ACT.Abs_reciprocal_sqrt)
 
         scalar_unread = held.tile([P, max(WIDTHS)], F32, name="scalar_unread")
-        vector_unread = held.tile([P, WIDTHS[-1]], F32, name="vector_unread")
         negshift = held.tile([P, 1], F32, name="negshift")
-        moments = psum.tile([P, 2], F32, name="moments")
+        m1 = psum.tile([P, 1], F32, name="m1")
+        m2 = psum.tile([P, 1], F32, name="m2")
 
         def statistics(i, t):
             first_chunk, last_chunk = i == 0, i == CHUNKS - 1
             unread = scalar_unread[:, 0 : WIDTHS[i]]
-            rowsums = held.tile([P, 2 * BLOCK], F32, name=f"rowsums{i}")
-            rowsum_d, rowsum_dd = rowsums[:, 0:1], rowsums[:, BLOCK : BLOCK + 1]
+            if not first_chunk:
+                rowsum_d = held.tile([P, 1], F32, name=f"rowsum_d{i}")
+            rowsum_dd = held.tile([P, 1], F32, name=f"rowsum_dd{i}")
             if first_chunk:
                 rowsum_t = held.tile([P, 1], F32, name="rowsum_t")
                 nc.scalar.activation(unread, t, ACT.Identity, accum_out=rowsum_t[:])
                 share = psum.tile([P, 1], F32, name="share")
                 average(share, rowsum_t[:], True, True)
                 nc.scalar.activation(negshift[:], share[:], ACT.Copy, scale=-1.0 * H / WIDTHS[0])
-                nc.gpsimd.memset(rowsums[:], 0.0)
-            elif last_chunk:
-                nc.vector.tensor_scalar(vector_unread[:], t, negshift[:], None, ADD, ADD, accum_out=rowsum_d)
+            elif i >= LAST_PAIR:
+                vector_unread = held.tile([P, WIDTHS[i]], F32, name=f"vector_unread{i}")
+                nc.vector.tensor_scalar(vector_unread[:], t, negshift[:], None, ADD, ADD, accum_out=rowsum_d[:])
             else:
-                nc.scalar.activation(unread, t, ACT.Identity, bias=negshift[:], accum_out=rowsum_d)
-            nc.scalar.activation(unread, t, ACT.Square, bias=negshift[:], accum_out=rowsum_dd)
-            both = rowsums[:].rearrange("p (m block) -> p m block", block=BLOCK)[:, :, 0]
-            average(moments, both, first_chunk, last_chunk)
+                nc.scalar.activation(unread, t, ACT.Identity, bias=negshift[:], accum_out=rowsum_d[:])
+            nc.scalar.activation(unread, t, ACT.Square, bias=negshift[:], accum_out=rowsum_dd[:])
+            if not first_chunk:
+                average(m1, rowsum_d[:], i == 1, last_chunk)
+            average(m2, rowsum_dd[:], first_chunk, last_chunk)
 
+        total = held.tile([P, H], F32, name="total")
         sums = [zeros[:, 0:width] for width in WIDTHS]
         for pair in range(0, CHUNKS, 2):
             for k in range(K):
                 for i in (pair, pair + 1):
                     column = (k * H + STARTS[i]) // 16
                     picked = table[:].indirect(offsets[:, column : column + WIDTHS[i] // 16])
-                    longer = held.tile([P, WIDTHS[i]], F32, name=f"t{i}_{k}")
-                    nc.vector.tensor_tensor(longer[:], picked, sums[i], ADD)
-                    sums[i] = longer[:]
+                    if k < K - 1:
+                        longer = held.tile([P, WIDTHS[i]], F32, name=f"t{i}_{k}")[:, 0 : WIDTHS[i]]
+                    else:
+                        longer = total[:, STARTS[i] : STARTS[i] + WIDTHS[i]]
+                    nc.vector.tensor_tensor(longer, picked, sums[i], ADD)
+                    sums[i] = longer
             statistics(pair, sums[pair])
             statistics(pair + 1, sums[pair + 1])
 
-        negvar = held.tile([P, 1], F32, name="negvar")
-        nc.vector.tensor_scalar(negvar[:], moments[:, 0:1], moments[:, 0:1], moments[:, 1:2], MULT, SUBTRACT)
+        negm1sq = held.tile([P, 1], F32, name="negm1sq")
+        nc.vector.tensor_scalar(negm1sq[:], m1[:], m1[:], -BESSEL, MULT, MULT)
         rstd = held.tile([P, 1], F32, name="rstd")
-        nc.scalar.activation(rstd[:], negvar[:], ACT.Abs_reciprocal_sqrt, scale=COUNT / (COUNT - 1))
+        nc.scalar.activation(rstd[:], m2[:], ACT.Abs_reciprocal_sqrt, bias=negm1sq[:], scale=BESSEL)
         negmu = held.tile([P, 1], F32, name="negmu")
-        nc.vector.tensor_tensor(negmu[:], negshift[:], moments[:, 0:1], SUBTRACT)
+        nc.vector.tensor_tensor(negmu[:], negshift[:], m1[:], SUBTRACT)
 
-        for i in reversed(range(CHUNKS)):
-            nc.vector.tensor_scalar(sums[i], sums[i], negmu[:], rstd[:], ADD, MULT)
-            nc.sync.dma_start(out[:, STARTS[i] : STARTS[i] + WIDTHS[i]], sums[i])
+        end = H
+        for width in PIECES:
+            piece = total[:, end - width : end]
+            nc.vector.tensor_scalar(piece, piece, negmu[:], rstd[:], ADD, MULT)
+            nc.sync.dma_start(out[:, end - width : end], piece)
+            end -= width

@@ -6,7 +6,7 @@ H = 2048
 K = 4
 COUNT = P * H
 BESSEL = COUNT / (COUNT - 1)
-WIDTHS = (640, 1024, 256, 128)
+WIDTHS = (576, 1024, 288, 160)
 LAST_PAIR = len(WIDTHS) - 2
 CHUNKS = len(WIDTHS)
 PIECES = (256, 384, 640, 768)
@@ -36,53 +36,58 @@ def tile_core_kernel(tc, cat, offs, out):
         def average(result, rowsums, start, stop):
             for q in range(0, P, QUADRANT):
                 nc.tensor.matmul(result[q : q + QUADRANT, :], averager[:], rowsums, start=start, stop=stop)
-        zeros = held.tile([P, max(WIDTHS)], F32, name="zeros")
+        zeros = held.tile([P, WIDTHS[0] + WIDTHS[1]], F32, name="zeros")
         nc.gpsimd.memset(zeros[:], 0.0)
         warm = held.tile([P, 1], F32, name="warm")
         nc.scalar.activation(warm[:], averager[:, 0:1], ACT.Abs_reciprocal_sqrt)
 
-        scalar_unread = held.tile([P, max(WIDTHS)], F32, name="scalar_unread")
         negshift = held.tile([P, 1], F32, name="negshift")
         m1 = psum.tile([P, 1], F32, name="m1")
         m2 = psum.tile([P, 1], F32, name="m2")
 
         def statistics(i, t):
             first_chunk, last_chunk = i == 0, i == CHUNKS - 1
-            unread = scalar_unread[:, 0 : WIDTHS[i]]
+            unread_t = held.tile([P, WIDTHS[i]], F32, name=f"unread_t{i}")
+            unread_dd = held.tile([P, WIDTHS[i]], F32, name=f"unread_dd{i}")
             if not first_chunk:
                 rowsum_d = held.tile([P, 1], F32, name=f"rowsum_d{i}")
             rowsum_dd = held.tile([P, 1], F32, name=f"rowsum_dd{i}")
             if first_chunk:
                 rowsum_t = held.tile([P, 1], F32, name="rowsum_t")
-                nc.scalar.activation(unread, t, ACT.Identity, accum_out=rowsum_t[:])
+                nc.scalar.activation(unread_t[:], t, ACT.Identity, accum_out=rowsum_t[:])
                 share = psum.tile([P, 1], F32, name="share")
                 average(share, rowsum_t[:], True, True)
                 nc.scalar.activation(negshift[:], share[:], ACT.Copy, scale=-1.0 * H / WIDTHS[0])
             elif i >= LAST_PAIR:
-                vector_unread = held.tile([P, WIDTHS[i]], F32, name=f"vector_unread{i}")
-                nc.vector.tensor_scalar(vector_unread[:], t, negshift[:], None, ADD, ADD, accum_out=rowsum_d[:])
+                nc.vector.tensor_scalar(unread_t[:], t, negshift[:], None, ADD, ADD, accum_out=rowsum_d[:])
             else:
-                nc.scalar.activation(unread, t, ACT.Identity, bias=negshift[:], accum_out=rowsum_d[:])
-            nc.scalar.activation(unread, t, ACT.Square, bias=negshift[:], accum_out=rowsum_dd[:])
+                nc.scalar.activation(unread_t[:], t, ACT.Identity, bias=negshift[:], accum_out=rowsum_d[:])
+            nc.scalar.activation(unread_dd[:], t, ACT.Square, bias=negshift[:], accum_out=rowsum_dd[:])
             if not first_chunk:
                 average(m1, rowsum_d[:], i == 1, last_chunk)
             average(m2, rowsum_dd[:], first_chunk, last_chunk)
 
-        total = held.tile([P, H], F32, name="total")
-        sums = [zeros[:, 0:width] for width in WIDTHS]
+        links = [held.tile([P, H], F32, name=f"link{k}") for k in range(K)]
+        total = links[K - 1]
+
+        def picked(k, first, width):
+            column = (k * H + first) // 16
+            return table[:].indirect(offsets[:, column : column + width // 16])
+
         for pair in range(0, CHUNKS, 2):
-            for k in range(K):
+            first, width = STARTS[pair], WIDTHS[pair] + WIDTHS[pair + 1]
+            nc.vector.tensor_tensor(
+                links[0][:, first : first + width], picked(0, first, width), zeros[:, 0:width], ADD
+            )
+        for pair in range(0, CHUNKS, 2):
+            for k in range(1, K):
                 for i in (pair, pair + 1):
-                    column = (k * H + STARTS[i]) // 16
-                    picked = table[:].indirect(offsets[:, column : column + WIDTHS[i] // 16])
-                    if k < K - 1:
-                        longer = held.tile([P, WIDTHS[i]], F32, name=f"t{i}_{k}")[:, 0 : WIDTHS[i]]
-                    else:
-                        longer = total[:, STARTS[i] : STARTS[i] + WIDTHS[i]]
-                    nc.vector.tensor_tensor(longer, picked, sums[i], ADD)
-                    sums[i] = longer
-            statistics(pair, sums[pair])
-            statistics(pair + 1, sums[pair + 1])
+                    nodes = slice(STARTS[i], STARTS[i] + WIDTHS[i])
+                    nc.vector.tensor_tensor(
+                        links[k][:, nodes], picked(k, STARTS[i], WIDTHS[i]), links[k - 1][:, nodes], ADD
+                    )
+            for i in (pair, pair + 1):
+                statistics(i, total[:, STARTS[i] : STARTS[i] + WIDTHS[i]])
 
         negm1sq = held.tile([P, 1], F32, name="negm1sq")
         nc.vector.tensor_scalar(negm1sq[:], m1[:], m1[:], -BESSEL, MULT, MULT)

@@ -11,6 +11,7 @@ LAST_PAIR = len(WIDTHS) - 2
 CHUNKS = len(WIDTHS)
 PIECES = (256, 384, 640, 768)
 STARTS = [sum(WIDTHS[:i]) for i in range(CHUNKS)]
+BLOCK = 8
 QUADRANT = 32
 
 F32 = mybir.dt.float32
@@ -42,30 +43,29 @@ def tile_core_kernel(tc, cat, offs, out):
         nc.scalar.activation(warm[:], averager[:, 0:1], ACT.Abs_reciprocal_sqrt)
 
         negshift = held.tile([P, 1], F32, name="negshift")
-        m1 = psum.tile([P, 1], F32, name="m1")
-        m2 = psum.tile([P, 1], F32, name="m2")
+        moments = psum.tile([P, 2], F32, name="moments")
+        m1, m2 = moments[:, 0:1], moments[:, 1:2]
 
         def statistics(i, t):
             first_chunk, last_chunk = i == 0, i == CHUNKS - 1
             unread_t = held.tile([P, WIDTHS[i]], F32, name=f"unread_t{i}")
             unread_dd = held.tile([P, WIDTHS[i]], F32, name=f"unread_dd{i}")
-            if not first_chunk:
-                rowsum_d = held.tile([P, 1], F32, name=f"rowsum_d{i}")
-            rowsum_dd = held.tile([P, 1], F32, name=f"rowsum_dd{i}")
+            rowsums = held.tile([P, 2 * BLOCK], F32, name=f"rowsums{i}")
+            rowsum_d, rowsum_dd = rowsums[:, 0:1], rowsums[:, BLOCK : BLOCK + 1]
             if first_chunk:
                 rowsum_t = held.tile([P, 1], F32, name="rowsum_t")
                 nc.scalar.activation(unread_t[:], t, ACT.Identity, accum_out=rowsum_t[:])
                 share = psum.tile([P, 1], F32, name="share")
                 average(share, rowsum_t[:], True, True)
                 nc.scalar.activation(negshift[:], share[:], ACT.Copy, scale=-1.0 * H / WIDTHS[0])
+                nc.gpsimd.memset(rowsum_d, 0.0)
             elif i >= LAST_PAIR:
-                nc.vector.tensor_scalar(unread_t[:], t, negshift[:], None, ADD, ADD, accum_out=rowsum_d[:])
+                nc.vector.tensor_scalar(unread_t[:], t, negshift[:], None, ADD, ADD, accum_out=rowsum_d)
             else:
-                nc.scalar.activation(unread_t[:], t, ACT.Identity, bias=negshift[:], accum_out=rowsum_d[:])
-            nc.scalar.activation(unread_dd[:], t, ACT.Square, bias=negshift[:], accum_out=rowsum_dd[:])
-            if not first_chunk:
-                average(m1, rowsum_d[:], i == 1, last_chunk)
-            average(m2, rowsum_dd[:], first_chunk, last_chunk)
+                nc.scalar.activation(unread_t[:], t, ACT.Identity, bias=negshift[:], accum_out=rowsum_d)
+            nc.scalar.activation(unread_dd[:], t, ACT.Square, bias=negshift[:], accum_out=rowsum_dd)
+            both = rowsums[:].rearrange("p (m block) -> p m block", block=BLOCK)[:, :, 0]
+            average(moments, both, first_chunk, last_chunk)
 
         links = [held.tile([P, H], F32, name=f"link{k}") for k in range(K)]
         total = links[K - 1]
@@ -89,12 +89,12 @@ def tile_core_kernel(tc, cat, offs, out):
             for i in (pair, pair + 1):
                 statistics(i, total[:, STARTS[i] : STARTS[i] + WIDTHS[i]])
 
-        negm1sq = held.tile([P, 1], F32, name="negm1sq")
-        nc.vector.tensor_scalar(negm1sq[:], m1[:], m1[:], -BESSEL, MULT, MULT)
+        negvar = held.tile([P, 1], F32, name="negvar")
+        nc.vector.tensor_scalar(negvar[:], m1, m1, m2, MULT, SUBTRACT)
         rstd = held.tile([P, 1], F32, name="rstd")
-        nc.scalar.activation(rstd[:], m2[:], ACT.Abs_reciprocal_sqrt, bias=negm1sq[:], scale=BESSEL)
+        nc.scalar.activation(rstd[:], negvar[:], ACT.Abs_reciprocal_sqrt, scale=BESSEL)
         negmu = held.tile([P, 1], F32, name="negmu")
-        nc.vector.tensor_tensor(negmu[:], negshift[:], m1[:], SUBTRACT)
+        nc.vector.tensor_tensor(negmu[:], negshift[:], m1, SUBTRACT)
 
         end = H
         for width in PIECES:

@@ -6,8 +6,9 @@ H = 2048
 K = 4
 COUNT = P * H
 BESSEL = COUNT / (COUNT - 1)
-WIDTHS = (576, 1024, 288, 160)
+WIDTHS = (608, 1024, 192, 224)
 LAST_PAIR = len(WIDTHS) - 2
+LAST_NODES = sum(WIDTHS[LAST_PAIR:])
 CHUNKS = len(WIDTHS)
 PIECES = (256, 384, 640, 768)
 STARTS = [sum(WIDTHS[:i]) for i in range(CHUNKS)]
@@ -48,7 +49,8 @@ def tile_core_kernel(tc, cat, offs, out):
 
         def statistics(i, t):
             first_chunk, last_chunk = i == 0, i == CHUNKS - 1
-            unread_t = held.tile([P, WIDTHS[i]], F32, name=f"unread_t{i}")
+            if i < LAST_PAIR:
+                unread_t = held.tile([P, WIDTHS[i]], F32, name=f"unread_t{i}")
             unread_dd = held.tile([P, WIDTHS[i]], F32, name=f"unread_dd{i}")
             rowsums = held.tile([P, 2 * BLOCK], F32, name=f"rowsums{i}")
             rowsum_d, rowsum_dd = rowsums[:, 0:1], rowsums[:, BLOCK : BLOCK + 1]
@@ -58,9 +60,9 @@ def tile_core_kernel(tc, cat, offs, out):
                 share = psum.tile([P, 1], F32, name="share")
                 average(share, rowsum_t[:], True, True)
                 nc.scalar.activation(negshift[:], share[:], ACT.Copy, scale=-1.0 * H / WIDTHS[0])
-                nc.gpsimd.memset(rowsum_d, 0.0)
+                nc.scalar.activation(rowsum_d, share[:], ACT.Copy, scale=-1.0 * H / WIDTHS[0] * LAST_NODES)
             elif i >= LAST_PAIR:
-                nc.vector.tensor_scalar(unread_t[:], t, negshift[:], None, ADD, ADD, accum_out=rowsum_d)
+                nc.vector.tensor_reduce(rowsum_d, t, axis=mybir.AxisListType.X, op=ADD)
             else:
                 nc.scalar.activation(unread_t[:], t, ACT.Identity, bias=negshift[:], accum_out=rowsum_d)
             nc.scalar.activation(unread_dd[:], t, ACT.Square, bias=negshift[:], accum_out=rowsum_dd)

@@ -55,12 +55,12 @@ def tile_core_kernel(tc, cat, offs, out):
             rowsums = held.tile([P, 2 * BLOCK], F32, name=f"rowsums{i}")
             rowsum_d, rowsum_dd = rowsums[:, 0:1], rowsums[:, BLOCK : BLOCK + 1]
             if first_chunk:
-                rowsum_t = held.tile([P, 1], F32, name="rowsum_t")
-                nc.scalar.activation(unread_t[:], t, ACT.Identity, accum_out=rowsum_t[:])
+                nc.scalar.activation(
+                    unread_t[:], t, ACT.Identity, scale=-LAST_NODES / WIDTHS[0], accum_out=rowsum_d
+                )
                 share = psum.tile([P, 1], F32, name="share")
-                average(share, rowsum_t[:], True, True)
-                nc.scalar.activation(negshift[:], share[:], ACT.Copy, scale=-1.0 * H / WIDTHS[0])
-                nc.scalar.activation(rowsum_d, share[:], ACT.Copy, scale=-1.0 * H / WIDTHS[0] * LAST_NODES)
+                average(share, rowsum_d, True, True)
+                nc.scalar.activation(negshift[:], share[:], ACT.Copy, scale=H / LAST_NODES)
             elif i >= LAST_PAIR:
                 nc.vector.tensor_reduce(rowsum_d, t, axis=mybir.AxisListType.X, op=ADD)
             else:

@@ -33,13 +33,13 @@ def tile_core_kernel(tc, cat, offs, out):
         nc.sync.dma_start(table[:, S // 2 : S], cat[:, S // 2 : S])
 
         averager = held.tile([P, QUADRANT], F32, name="averager")
-        nc.gpsimd.memset(averager[:], 1.0 / COUNT)
+        nc.vector.memset(averager[:], 1.0 / COUNT)
 
         def average(result, rowsums, start, stop):
             for q in range(0, P, QUADRANT):
                 nc.tensor.matmul(result[q : q + QUADRANT, :], averager[:], rowsums, start=start, stop=stop)
         zeros = held.tile([P, WIDTHS[0] + WIDTHS[1]], F32, name="zeros")
-        nc.gpsimd.memset(zeros[:], 0.0)
+        nc.vector.memset(zeros[:], 0.0)
         warm = held.tile([P, 1], F32, name="warm")
         nc.scalar.activation(warm[:], averager[:, 0:1], ACT.Abs_reciprocal_sqrt)
 

import concourse.mybir as mybir

P = 128
S = 4096
H = 2048
K = 4
COUNT = P * H
BESSEL = COUNT / (COUNT - 1)
WIDTHS = (608, 1024, 192, 224)
LAST_PAIR = len(WIDTHS) - 2
LAST_NODES = sum(WIDTHS[LAST_PAIR:])
CHUNKS = len(WIDTHS)
PIECES = (256, 384, 640, 768)
STARTS = [sum(WIDTHS[:i]) for i in range(CHUNKS)]
BLOCK = 8
QUADRANT = 32

F32 = mybir.dt.float32
U16 = mybir.dt.uint16
ADD = mybir.AluOpType.add
SUBTRACT = mybir.AluOpType.subtract
MULT = mybir.AluOpType.mult
ACT = mybir.ActivationFunctionType


def tile_core_kernel(tc, cat, offs, out):
    nc = tc.nc
    with tc.tile_pool(name="held", bufs=1) as held, tc.psum_pool(name="psum", bufs=1) as psum:
        offsets = held.tile([P, K * H // 16], U16, name="offsets")
        nc.sync.dma_start(offsets[:], offs)
        table = held.tile([P, S], F32, name="table")
        nc.scalar.dma_start(table[:, 0 : S // 2], cat[:, 0 : S // 2])
        nc.sync.dma_start(table[:, S // 2 : S], cat[:, S // 2 : S])

        averager = held.tile([P, QUADRANT], F32, name="averager")
        nc.vector.memset(averager[:], 1.0 / COUNT)

        def average(result, rowsums, start, stop):
            for q in range(0, P, QUADRANT):
                nc.tensor.matmul(result[q : q + QUADRANT, :], averager[:], rowsums, start=start, stop=stop)
        zeros = held.tile([P, WIDTHS[0] + WIDTHS[1]], F32, name="zeros")
        nc.vector.memset(zeros[:], 0.0)
        warm = held.tile([P, 1], F32, name="warm")
        nc.scalar.activation(warm[:], averager[:, 0:1], ACT.Abs_reciprocal_sqrt)

        negshift = held.tile([P, 1], F32, name="negshift")
        moments = psum.tile([P, 2], F32, name="moments")
        m1, m2 = moments[:, 0:1], moments[:, 1:2]

        def statistics(i, t):
            first_chunk, last_chunk = i == 0, i == CHUNKS - 1
            if i < LAST_PAIR:
                unread_t = held.tile([P, WIDTHS[i]], F32, name=f"unread_t{i}")
            unread_dd = held.tile([P, WIDTHS[i]], F32, name=f"unread_dd{i}")
            rowsums = held.tile([P, 2 * BLOCK], F32, name=f"rowsums{i}")
            rowsum_d, rowsum_dd = rowsums[:, 0:1], rowsums[:, BLOCK : BLOCK + 1]
            if first_chunk:
                nc.scalar.activation(
                    unread_t[:], t, ACT.Identity, scale=-LAST_NODES / WIDTHS[0], accum_out=rowsum_d
                )
                share = psum.tile([P, 1], F32, name="share")
                average(share, rowsum_d, True, True)
                nc.scalar.activation(negshift[:], share[:], ACT.Copy, scale=H / LAST_NODES)
            elif i >= LAST_PAIR:
                nc.vector.tensor_reduce(rowsum_d, t, axis=mybir.AxisListType.X, op=ADD)
            else:
                nc.scalar.activation(unread_t[:], t, ACT.Identity, bias=negshift[:], accum_out=rowsum_d)
            nc.scalar.activation(unread_dd[:], t, ACT.Square, bias=negshift[:], accum_out=rowsum_dd)
            both = rowsums[:].rearrange("p (m block) -> p m block", block=BLOCK)[:, :, 0]
            average(moments, both, first_chunk, last_chunk)

        links = [held.tile([P, H], F32, name=f"link{k}") for k in range(K)]
        total = links[K - 1]

        def picked(k, first, width):
            column = (k * H + first) // 16
            return table[:].indirect(offsets[:, column : column + width // 16])

        for pair in range(0, CHUNKS, 2):
            first, width = STARTS[pair], WIDTHS[pair] + WIDTHS[pair + 1]
            nc.vector.tensor_tensor(
                links[0][:, first : first + width], picked(0, first, width), zeros[:, 0:width], ADD
            )
        for pair in range(0, CHUNKS, 2):
            for k in range(1, K):
                for i in (pair, pair + 1):
                    nodes = slice(STARTS[i], STARTS[i] + WIDTHS[i])
                    nc.vector.tensor_tensor(
                        links[k][:, nodes], picked(k, STARTS[i], WIDTHS[i]), links[k - 1][:, nodes], ADD
                    )
            for i in (pair, pair + 1):
                statistics(i, total[:, STARTS[i] : STARTS[i] + WIDTHS[i]])

        negvar = held.tile([P, 1], F32, name="negvar")
        nc.vector.tensor_scalar(negvar[:], m1, m1, m2, MULT, SUBTRACT)
        rstd = held.tile([P, 1], F32, name="rstd")
        nc.scalar.activation(rstd[:], negvar[:], ACT.Abs_reciprocal_sqrt, scale=BESSEL)
        negmu = held.tile([P, 1], F32, name="negmu")
        nc.vector.tensor_tensor(negmu[:], negshift[:], m1, SUBTRACT)

        end = H
        for width in PIECES:
            piece = total[:, end - width : end]
            nc.vector.tensor_scalar(piece, piece, negmu[:], rstd[:], ADD, MULT)
            nc.sync.dma_start(out[:, end - width : end], piece)
            end -= width
